import numpy as np
import ml_dtypes


def mxq(x, axis, fmt="e4m3"):
    dtype, down = {"e4m3": (ml_dtypes.float8_e4m3fn, 7), "e5m2": (ml_dtypes.float8_e5m2, 14)}[fmt]
    v = np.moveaxis(np.asarray(x, np.float32).astype(ml_dtypes.bfloat16).astype(np.float64), axis, -1)
    blocks = v.reshape(v.shape[:-1] + (-1, 32))
    amax = np.abs(blocks).max(-1, keepdims=True)
    byte = np.maximum(np.where(amax > 0, np.frexp(amax)[1] - 1 + 127, 0) - down, 1)
    scale = np.exp2(byte - 127.0)
    codes = (blocks / scale).astype(np.float32).astype(dtype).astype(np.float64)
    return np.moveaxis((codes * scale).reshape(v.shape), -1, axis)


WIDE = False


def mx_kscale(k):
    if not WIDE:
        return np.ones(k)
    levels = np.array([10, -10, 5, -5, 0])
    a = np.random.permutation(np.resize(levels, k // 512 * 4)).reshape(k // 512, 4)
    idx = np.arange(k)
    return np.exp2(a[idx // 512, idx % 128 // 32])


BF16 = ml_dtypes.bfloat16


def bf(x):
    return np.asarray(x, np.float32).astype(BF16)


def f64(x):
    return np.asarray(x).astype(np.float64)


B, C, H, W = 1, 512, 32, 32
N = H * W
SIG = 3.0


def setup_inputs():
    s, t = mx_kscale(C), mx_kscale(C)
    r = np.sqrt(SIG / np.sqrt(C))
    return {
        "q_ir": bf(np.random.standard_normal((B, C, N)) * r / t[:, None]),
        "irSegF": bf(np.random.standard_normal((B, C, H, W)) * s[:, None, None]),
        "Wk_dr": bf(np.random.standard_normal((C, C)) * r / np.sqrt(C) * t[:, None] / s[None, :]),
        "bk_dr": bf(np.random.standard_normal(C) * 0.1 * t),
    }


def reference(q_ir, irSegF, Wk_dr, bk_dr):
    seg = f64(irSegF).reshape(B, C, N)
    key = (mxq(f64(Wk_dr), 1, "e4m3") @ mxq(seg, 1, "e4m3")) + f64(bk_dr)[None, :, None]
    s = mxq(f64(q_ir), 1, "e4m3").transpose(0, 2, 1) @ mxq(key, 1, "e4m3")
    e = np.exp(s - s.max(1, keepdims=True))
    return e / e.sum(1, keepdims=True)

@@ -1,0 +1,198 @@
+from contextlib import ExitStack
+
+import concourse.masks as masks
+import concourse.mybir as mybir
+
+BF16 = mybir.dt.bfloat16
+F32 = mybir.dt.float32
+U32 = mybir.dt.uint32
+U8 = mybir.dt.uint8
+FP8X4 = mybir.dt.float8_e4m3fn_x4
+ALU = mybir.AluOpType
+ACT = mybir.ActivationFunctionType
+AXIS = mybir.AxisListType
+
+P = 128
+PACK = 4
+C = P * PACK
+N = 1024
+BANK = 512
+HALVES = N // BANK
+M_TILES = N // P
+N_TILES_PER_BANK = BANK // P
+RUN = 4
+
+FLOPS = 2 * C * C * N + 2 * N * N * C
+
+
+def regroup(copy, grouped, rows):
+    copy(
+        out=grouped.rearrange("p (c i) j -> p c j i", i=RUN),
+        in_=rows.rearrange("p j (c i) -> p c j i", i=RUN),
+    )
+
+
+def tile_featuremaptransformer_pb_kernel(tc, q_ir, irSegF, Wk_dr, bk_dr, out):
+    nc = tc.nc
+    with ExitStack() as ctx:
+        keep = ctx.enter_context(tc.tile_pool(name="keep", bufs=1))
+        stats = ctx.enter_context(tc.tile_pool(name="stats", bufs=4))
+        rows_pool = ctx.enter_context(tc.tile_pool(name="rows", bufs=3))
+        psum = ctx.enter_context(tc.psum_pool(name="psum", bufs=4))
+
+        w_rows = keep.tile([P, PACK * C], BF16)
+        seg_rows = keep.tile([P, PACK, N], BF16)
+        q_rows = keep.tile([P, PACK, N], BF16)
+        bias = keep.tile([P, PACK], BF16)
+        seg_dram = irSegF[0].rearrange("(p j) h w -> p j (h w)", j=PACK)
+        q_dram = q_ir[0].rearrange("(p j) n -> p j n", j=PACK)
+        half_cols = [slice(h * BANK, (h + 1) * BANK) for h in range(HALVES)]
+        nc.sync.dma_start(out=w_rows[:], in_=Wk_dr.rearrange("(p t) c -> p (t c)", t=PACK))
+        nc.scalar.dma_start(out=bias[:], in_=bk_dr.rearrange("(p t) -> p t", t=PACK))
+        nc.sync.dma_start(out=seg_rows[:, :, half_cols[0]], in_=seg_dram[:, :, half_cols[0]])
+        for h in range(HALVES):
+            nc.sync.dma_start(out=q_rows[:, :, half_cols[h]], in_=q_dram[:, :, half_cols[h]])
+        nc.sync.dma_start(out=seg_rows[:, :, half_cols[1]], in_=seg_dram[:, :, half_cols[1]])
+
+        identity = keep.tile([P, P], F32)
+        masks.make_identity(nc, identity[:])
+
+        warm = keep.tile([P, 1], F32)
+        nc.vector.memset(warm[:], 0.0)
+        nc.scalar.activation(out=warm[:], in_=warm[:], func=ACT.Exp)
+
+        w_words = w_rows[:].bitcast(F32).rearrange("o (t p u) -> o t u p", t=PACK, u=2)
+        w_grouped = keep.tile([P, PACK * P * PACK], BF16, align_bytes=64)
+        w_grouped_words = w_grouped[:].bitcast(F32).rearrange("p (t o u) -> p t o u", t=PACK, u=2)
+        w_codes = keep.tile([P, PACK * P], U32, align_bytes=64)
+        w_scales = keep.tile([P, PACK * P], U8, align_bytes=64)
+        for b in range(2):
+            w_t = psum.tile([P, 2, 2, P], F32, tag="work")
+            for t in range(2):
+                for u in range(2):
+                    nc.tensor.transpose(w_t[:, t, u, :], w_words[:, 2 * b + t, u, :], identity[:])
+            nc.scalar.copy(
+                out=w_grouped_words[:, 2 * b : 2 * b + 2, :, :],
+                in_=w_t[:].rearrange("p t u o -> p t o u"),
+            )
+        nc.vector.quantize_mx(out=w_codes[:].bitcast(FP8X4), scales=w_scales[:], in_=w_grouped[:])
+
+        q_grouped = keep.tile([P, N, PACK], BF16, align_bytes=64)
+        q_codes = keep.tile([P, N], U32, align_bytes=64)
+        q_scales = keep.tile([P, N], U8, align_bytes=64)
+        regroup(nc.scalar.copy, q_grouped[:, half_cols[0], :], q_rows[:, :, half_cols[0]])
+        regroup(nc.vector.tensor_copy, q_grouped[:, half_cols[1], :], q_rows[:, :, half_cols[1]])
+
+        seg_grouped = keep.tile([P, N, PACK], BF16, align_bytes=64)
+        seg_codes = keep.tile([P, N], U32, align_bytes=64)
+        seg_scales = keep.tile([P, N], U8, align_bytes=64)
+        key_grouped = keep.tile([P, N, PACK], BF16, align_bytes=64)
+        key_codes = keep.tile([P, N], U32, align_bytes=64)
+        key_scales = keep.tile([P, N], U8, align_bytes=64)
+        out_dram = out[0].rearrange("(j p) m -> p j m", p=P)
+        weights = {}
+
+        def m_cols(i):
+            return slice(i * P, (i + 1) * P)
+
+        def regroup_seg(i):
+            regroup(nc.vector.tensor_copy, seg_grouped[:, m_cols(i), :], seg_rows[:, :, m_cols(i)])
+
+        def project_keys(i):
+            nc.vector.quantize_mx(
+                out=seg_codes[:, m_cols(i)].bitcast(FP8X4),
+                scales=seg_scales[:, m_cols(i)],
+                in_=seg_grouped[:, m_cols(i), :].rearrange("p m j -> p (m j)"),
+            )
+            key_bank = psum.tile([P, PACK, P], F32, tag="work")
+            for t in range(PACK):
+                nc.tensor.matmul_mx(
+                    out=key_bank[:, t, :],
+                    lhsT=w_codes[:, t * P : (t + 1) * P].bitcast(FP8X4),
+                    lhsT_scale=w_scales[:, t * P : (t + 1) * P],
+                    rhs=seg_codes[:, m_cols(i)].bitcast(FP8X4),
+                    rhs_scale=seg_scales[:, m_cols(i)],
+                    start=True,
+                    stop=True,
+                )
+            nc.vector.tensor_tensor(
+                out=key_grouped[:, m_cols(i), :],
+                in0=key_bank[:].rearrange("p t m -> p m t"),
+                in1=bias[:].unsqueeze(1).to_broadcast([P, P, PACK]),
+                op=ALU.add,
+            )
+
+        def softmax_over_queries(i):
+            nc.vector.quantize_mx(
+                out=key_codes[:, m_cols(i)].bitcast(FP8X4),
+                scales=key_scales[:, m_cols(i)],
+                in_=key_grouped[:, m_cols(i), :].rearrange("p m t -> p (m t)"),
+            )
+            half_max = stats.tile([P, HALVES], F32)
+            half_sum = stats.tile([P, HALVES], F32)
+            neg_max = stats.tile([P, 1], F32)
+            total = stats.tile([P, 1], F32)
+            scale = stats.tile([P, 1], F32)
+            e = rows_pool.tile([P, N], F32)
+            scores = []
+            for h in range(HALVES):
+                score = psum.tile([P, BANK], F32, tag="score")
+                nc.tensor.matmul_mx(
+                    out=score[:],
+                    lhsT=key_codes[:, m_cols(i)].bitcast(FP8X4),
+                    lhsT_scale=key_scales[:, m_cols(i)],
+                    rhs=q_codes[:, half_cols[h]].bitcast(FP8X4),
+                    rhs_scale=q_scales[:, half_cols[h]],
+                    start=True,
+                    stop=True,
+                )
+                nc.vector.tensor_reduce(out=half_max[:, h : h + 1], in_=score[:], axis=AXIS.X, op=ALU.max)
+                scores.append(score)
+            nc.vector.tensor_reduce(out=neg_max[:], in_=half_max[:], axis=AXIS.X, op=ALU.max, negate=True)
+            for h in range(HALVES):
+                nc.scalar.activation(
+                    out=e[:, half_cols[h]],
+                    in_=scores[h][:],
+                    func=ACT.Exp,
+                    bias=neg_max[:],
+                    scale=1.0,
+                    accum_out=half_sum[:, h : h + 1],
+                )
+            nc.vector.tensor_reduce(out=total[:], in_=half_sum[:], axis=AXIS.X, op=ALU.add)
+            nc.vector.reciprocal(out=scale[:], in_=total[:])
+            weights[i] = (e, scale)
+
+        def store_transposed(i):
+            e, scale = weights[i]
+            for h in range(HALVES):
+                nc.gpsimd.tensor_scalar(
+                    out=e[:, half_cols[h]],
+                    in0=e[:, half_cols[h]],
+                    scalar1=scale[:],
+                    scalar2=0.0,
+                    op0=ALU.mult,
+                    op1=ALU.add,
+                )
+                flipped = psum.tile([P, N_TILES_PER_BANK, P], F32, tag="work")
+                for j in range(N_TILES_PER_BANK):
+                    n_tile = h * N_TILES_PER_BANK + j
+                    nc.tensor.transpose(flipped[:, j, :], e[:, n_tile * P : (n_tile + 1) * P], identity[:])
+                staged = rows_pool.tile([P, N_TILES_PER_BANK, P], F32)
+                nc.scalar.copy(out=staged[:], in_=flipped[:])
+                n_tiles = slice(h * N_TILES_PER_BANK, (h + 1) * N_TILES_PER_BANK)
+                nc.sync.dma_start(out=out_dram[:, n_tiles, m_cols(i)], in_=staged[:])
+
+        regroup_seg(0)
+        for h in range(HALVES):
+            nc.vector.quantize_mx(
+                out=q_codes[:, half_cols[h]].bitcast(FP8X4),
+                scales=q_scales[:, half_cols[h]],
+                in_=q_grouped[:, half_cols[h], :].rearrange("p n j -> p (n j)"),
+            )
+
+        stages = (regroup_seg, project_keys, softmax_over_queries, store_transposed)
+        for step in range(1, M_TILES + len(stages) - 1):
+            for lag, stage in enumerate(stages):
+                i = step - lag
+                if 0 <= i < M_TILES:
+                    stage(i)

@@ -35,9 +35,10 @@ def regroup(copy, grouped, rows):
 def tile_featuremaptransformer_pb_kernel(tc, q_ir, irSegF, Wk_dr, bk_dr, out):
     nc = tc.nc
     with ExitStack() as ctx:
+        ctx.enter_context(tc.manual_schedule())
         keep = ctx.enter_context(tc.tile_pool(name="keep", bufs=1))
         stats = ctx.enter_context(tc.tile_pool(name="stats", bufs=4))
-        rows_pool = ctx.enter_context(tc.tile_pool(name="rows", bufs=3))
+        rows_pool = ctx.enter_context(tc.tile_pool(name="rows", bufs=4))
         psum = ctx.enter_context(tc.psum_pool(name="psum", bufs=4))
 
         w_rows = keep.tile([P, PACK * C], BF16)
@@ -75,14 +76,10 @@ def tile_featuremaptransformer_pb_kernel(tc, q_ir, irSegF, Wk_dr, bk_dr, out):
                 out=w_grouped_words[:, 2 * b : 2 * b + 2, :, :],
                 in_=w_t[:].rearrange("p t u o -> p t o u"),
             )
-        nc.vector.quantize_mx(out=w_codes[:].bitcast(FP8X4), scales=w_scales[:], in_=w_grouped[:])
 
         q_grouped = keep.tile([P, N, PACK], BF16, align_bytes=64)
         q_codes = keep.tile([P, N], U32, align_bytes=64)
         q_scales = keep.tile([P, N], U8, align_bytes=64)
-        regroup(nc.scalar.copy, q_grouped[:, half_cols[0], :], q_rows[:, :, half_cols[0]])
-        regroup(nc.vector.tensor_copy, q_grouped[:, half_cols[1], :], q_rows[:, :, half_cols[1]])
-
         seg_grouped = keep.tile([P, N, PACK], BF16, align_bytes=64)
         seg_codes = keep.tile([P, N], U32, align_bytes=64)
         seg_scales = keep.tile([P, N], U8, align_bytes=64)
@@ -90,13 +87,10 @@ def tile_featuremaptransformer_pb_kernel(tc, q_ir, irSegF, Wk_dr, bk_dr, out):
         key_codes = keep.tile([P, N], U32, align_bytes=64)
         key_scales = keep.tile([P, N], U8, align_bytes=64)
         out_dram = out[0].rearrange("(j p) m -> p j m", p=P)
-        weights = {}
+        live = {}
 
         def m_cols(i):
             return slice(i * P, (i + 1) * P)
-
-        def regroup_seg(i):
-            regroup(nc.vector.tensor_copy, seg_grouped[:, m_cols(i), :], seg_rows[:, :, m_cols(i)])
 
         def project_keys(i):
             nc.vector.quantize_mx(
@@ -115,30 +109,26 @@ def tile_featuremaptransformer_pb_kernel(tc, q_ir, irSegF, Wk_dr, bk_dr, out):
                     start=True,
                     stop=True,
                 )
+            live["key_bank", i] = key_bank
+
+        def add_bias(i):
             nc.vector.tensor_tensor(
                 out=key_grouped[:, m_cols(i), :],
-                in0=key_bank[:].rearrange("p t m -> p m t"),
+                in0=live["key_bank", i][:].rearrange("p t m -> p m t"),
                 in1=bias[:].unsqueeze(1).to_broadcast([P, P, PACK]),
                 op=ALU.add,
             )
 
-        def softmax_over_queries(i):
+        def score(i):
             nc.vector.quantize_mx(
                 out=key_codes[:, m_cols(i)].bitcast(FP8X4),
                 scales=key_scales[:, m_cols(i)],
                 in_=key_grouped[:, m_cols(i), :].rearrange("p m t -> p (m t)"),
             )
-            half_max = stats.tile([P, HALVES], F32)
-            half_sum = stats.tile([P, HALVES], F32)
-            neg_max = stats.tile([P, 1], F32)
-            total = stats.tile([P, 1], F32)
-            scale = stats.tile([P, 1], F32)
-            e = rows_pool.tile([P, N], F32)
-            scores = []
             for h in range(HALVES):
-                score = psum.tile([P, BANK], F32, tag="score")
+                score_bank = psum.tile([P, BANK], F32, tag="score")
                 nc.tensor.matmul_mx(
-                    out=score[:],
+                    out=score_bank[:],
                     lhsT=key_codes[:, m_cols(i)].bitcast(FP8X4),
                     lhsT_scale=key_scales[:, m_cols(i)],
                     rhs=q_codes[:, half_cols[h]].bitcast(FP8X4),
@@ -146,43 +136,79 @@ def tile_featuremaptransformer_pb_kernel(tc, q_ir, irSegF, Wk_dr, bk_dr, out):
                     start=True,
                     stop=True,
                 )
-                nc.vector.tensor_reduce(out=half_max[:, h : h + 1], in_=score[:], axis=AXIS.X, op=ALU.max)
-                scores.append(score)
-            nc.vector.tensor_reduce(out=neg_max[:], in_=half_max[:], axis=AXIS.X, op=ALU.max, negate=True)
+                live["score", i, h] = score_bank
+
+        def max_of_halves(i):
+            half_max = stats.tile([P, HALVES], F32)
+            for h in range(HALVES):
+                nc.vector.tensor_reduce(
+                    out=half_max[:, h : h + 1], in_=live["score", i, h][:], axis=AXIS.X, op=ALU.max
+                )
+            live["half_max", i] = half_max
+
+        def negated_max(i):
+            neg_max = stats.tile([P, 1], F32)
+            nc.vector.tensor_reduce(
+                out=neg_max[:], in_=live["half_max", i][:], axis=AXIS.X, op=ALU.max, negate=True
+            )
+            live["neg_max", i] = neg_max
+
+        def exponentials(i):
+            e = rows_pool.tile([P, N], F32)
+            half_sum = stats.tile([P, HALVES], F32)
             for h in range(HALVES):
                 nc.scalar.activation(
                     out=e[:, half_cols[h]],
-                    in_=scores[h][:],
+                    in_=live["score", i, h][:],
                     func=ACT.Exp,
-                    bias=neg_max[:],
+                    bias=live["neg_max", i][:],
                     scale=1.0,
                     accum_out=half_sum[:, h : h + 1],
                 )
-            nc.vector.tensor_reduce(out=total[:], in_=half_sum[:], axis=AXIS.X, op=ALU.add)
-            nc.vector.reciprocal(out=scale[:], in_=total[:])
-            weights[i] = (e, scale)
+            live["e", i] = e
+            live["half_sum", i] = half_sum
 
-        def store_transposed(i):
-            e, scale = weights[i]
+        def sum_of_halves(i):
+            total = stats.tile([P, 1], F32)
+            nc.vector.tensor_reduce(out=total[:], in_=live["half_sum", i][:], axis=AXIS.X, op=ALU.add)
+            live["total", i] = total
+
+        def normalise(i):
+            inverse = stats.tile([P, 1], F32)
+            nc.vector.reciprocal(out=inverse[:], in_=live["total", i][:])
+            e = live["e", i]
             for h in range(HALVES):
                 nc.gpsimd.tensor_scalar(
                     out=e[:, half_cols[h]],
                     in0=e[:, half_cols[h]],
-                    scalar1=scale[:],
+                    scalar1=inverse[:],
                     scalar2=0.0,
                     op0=ALU.mult,
                     op1=ALU.add,
                 )
+
+        def flip(i):
+            e = live["e", i]
+            for h in range(HALVES):
                 flipped = psum.tile([P, N_TILES_PER_BANK, P], F32, tag="work")
                 for j in range(N_TILES_PER_BANK):
                     n_tile = h * N_TILES_PER_BANK + j
                     nc.tensor.transpose(flipped[:, j, :], e[:, n_tile * P : (n_tile + 1) * P], identity[:])
+                live["flipped", i, h] = flipped
+
+        def store(i):
+            for h in range(HALVES):
                 staged = rows_pool.tile([P, N_TILES_PER_BANK, P], F32)
-                nc.scalar.copy(out=staged[:], in_=flipped[:])
+                nc.scalar.copy(out=staged[:], in_=live["flipped", i, h][:])
                 n_tiles = slice(h * N_TILES_PER_BANK, (h + 1) * N_TILES_PER_BANK)
                 nc.sync.dma_start(out=out_dram[:, n_tiles, m_cols(i)], in_=staged[:])
 
-        regroup_seg(0)
+        regroup(nc.vector.tensor_copy, seg_grouped[:, half_cols[0], :], seg_rows[:, :, half_cols[0]])
+        regroup(nc.scalar.copy, q_grouped[:, half_cols[0], :], q_rows[:, :, half_cols[0]])
+        nc.vector.quantize_mx(out=w_codes[:].bitcast(FP8X4), scales=w_scales[:], in_=w_grouped[:])
+        project_keys(0)
+        regroup(nc.vector.tensor_copy, q_grouped[:, half_cols[1], :], q_rows[:, :, half_cols[1]])
+        regroup(nc.scalar.copy, seg_grouped[:, half_cols[1], :], seg_rows[:, :, half_cols[1]])
         for h in range(HALVES):
             nc.vector.quantize_mx(
                 out=q_codes[:, half_cols[h]].bitcast(FP8X4),
@@ -190,9 +216,18 @@ def tile_featuremaptransformer_pb_kernel(tc, q_ir, irSegF, Wk_dr, bk_dr, out):
                 in_=q_grouped[:, half_cols[h], :].rearrange("p n j -> p (n j)"),
             )
 
-        stages = (regroup_seg, project_keys, softmax_over_queries, store_transposed)
-        for step in range(1, M_TILES + len(stages) - 1):
-            for lag, stage in enumerate(stages):
-                i = step - lag
-                if 0 <= i < M_TILES:
-                    stage(i)
+        def at(stage, i):
+            if 0 <= i < M_TILES:
+                stage(i)
+
+        for s in range(-2, M_TILES + 1):
+            at(flip, s - 1)
+            at(add_bias, s + 2)
+            at(project_keys, s + 3)
+            at(max_of_halves, s + 1)
+            at(exponentials, s)
+            at(sum_of_halves, s)
+            at(score, s + 2)
+            at(negated_max, s + 1)
+            at(normalise, s)
+            at(store, s - 1)

@@ -19,7 +19,9 @@ N = 1024
 BANK = 512
 HALVES = N // BANK
 M_TILES = N // P
+TILES_PER_HALF = M_TILES // HALVES
 N_TILES_PER_BANK = BANK // P
+FIRST_SHARED_TILE = 4
 RUN = 4
 
 FLOPS = 2 * C * C * N + 2 * N * N * C
@@ -39,7 +41,10 @@ def tile_featuremaptransformer_pb_kernel(tc, q_ir, irSegF, Wk_dr, bk_dr, out):
         keep = ctx.enter_context(tc.tile_pool(name="keep", bufs=1))
         stats = ctx.enter_context(tc.tile_pool(name="stats", bufs=4))
         rows_pool = ctx.enter_context(tc.tile_pool(name="rows", bufs=4))
-        psum = ctx.enter_context(tc.psum_pool(name="psum", bufs=4))
+        staging = ctx.enter_context(tc.tile_pool(name="staging", bufs=6))
+        score_banks = ctx.enter_context(tc.psum_pool(name="score_banks", bufs=4))
+        key_banks = ctx.enter_context(tc.psum_pool(name="key_banks", bufs=2))
+        flip_banks = ctx.enter_context(tc.psum_pool(name="flip_banks", bufs=2))
 
         w_rows = keep.tile([P, PACK * C], BF16)
         seg_rows = keep.tile([P, PACK, N], BF16)
@@ -68,7 +73,7 @@ def tile_featuremaptransformer_pb_kernel(tc, q_ir, irSegF, Wk_dr, bk_dr, out):
         w_codes = keep.tile([P, PACK * P], U32, align_bytes=64)
         w_scales = keep.tile([P, PACK * P], U8, align_bytes=64)
         for b in range(2):
-            w_t = psum.tile([P, 2, 2, P], F32, tag="work")
+            w_t = flip_banks.tile([P, 2, 2, P], F32, tag="flip")
             for t in range(2):
                 for u in range(2):
                     nc.tensor.transpose(w_t[:, t, u, :], w_words[:, 2 * b + t, u, :], identity[:])
@@ -92,13 +97,19 @@ def tile_featuremaptransformer_pb_kernel(tc, q_ir, irSegF, Wk_dr, bk_dr, out):
         def m_cols(i):
             return slice(i * P, (i + 1) * P)
 
-        def project_keys(i):
+        def quantise(codes, scales, grouped, cols):
             nc.vector.quantize_mx(
-                out=seg_codes[:, m_cols(i)].bitcast(FP8X4),
-                scales=seg_scales[:, m_cols(i)],
-                in_=seg_grouped[:, m_cols(i), :].rearrange("p m j -> p (m j)"),
+                out=codes[:, cols].bitcast(FP8X4),
+                scales=scales[:, cols],
+                in_=grouped[:, cols, :].rearrange("p w j -> p (w j)"),
             )
-            key_bank = psum.tile([P, PACK, P], F32, tag="work")
+
+        def quantise_seg(i):
+            if i % TILES_PER_HALF == 0:
+                quantise(seg_codes, seg_scales, seg_grouped, half_cols[i // TILES_PER_HALF])
+
+        def project_keys(i):
+            key_bank = key_banks.tile([P, PACK, P], F32, tag="key")
             for t in range(PACK):
                 nc.tensor.matmul_mx(
                     out=key_bank[:, t, :],
@@ -120,13 +131,9 @@ def tile_featuremaptransformer_pb_kernel(tc, q_ir, irSegF, Wk_dr, bk_dr, out):
             )
 
         def score(i):
-            nc.vector.quantize_mx(
-                out=key_codes[:, m_cols(i)].bitcast(FP8X4),
-                scales=key_scales[:, m_cols(i)],
-                in_=key_grouped[:, m_cols(i), :].rearrange("p m t -> p (m t)"),
-            )
+            quantise(key_codes, key_scales, key_grouped, m_cols(i))
             for h in range(HALVES):
-                score_bank = psum.tile([P, BANK], F32, tag="score")
+                score_bank = score_banks.tile([P, BANK], F32, tag="score")
                 nc.tensor.matmul_mx(
                     out=score_bank[:],
                     lhsT=key_codes[:, m_cols(i)].bitcast(FP8X4),
@@ -138,49 +145,47 @@ def tile_featuremaptransformer_pb_kernel(tc, q_ir, irSegF, Wk_dr, bk_dr, out):
                 )
                 live["score", i, h] = score_bank
 
-        def max_of_halves(i):
-            half_max = stats.tile([P, HALVES], F32)
+        def evacuate(i):
+            row = rows_pool.tile([P, N], F32)
+            half_min = stats.tile([P, HALVES], F32)
             for h in range(HALVES):
-                nc.vector.tensor_reduce(
-                    out=half_max[:, h : h + 1], in_=live["score", i, h][:], axis=AXIS.X, op=ALU.max
+                nc.vector.tensor_scalar(
+                    out=row[:, half_cols[h]],
+                    in0=live["score", i, h][:],
+                    scalar1=-1.0,
+                    scalar2=None,
+                    op0=ALU.mult,
+                    op1=ALU.min,
+                    accum_out=half_min[:, h : h + 1],
                 )
-            live["half_max", i] = half_max
+            live["row", i] = row
+            live["half_min", i] = half_min
 
         def negated_max(i):
             neg_max = stats.tile([P, 1], F32)
-            nc.vector.tensor_reduce(
-                out=neg_max[:], in_=live["half_max", i][:], axis=AXIS.X, op=ALU.max, negate=True
-            )
+            nc.vector.tensor_reduce(out=neg_max[:], in_=live["half_min", i][:], axis=AXIS.X, op=ALU.min)
             live["neg_max", i] = neg_max
 
         def exponentials(i):
-            e = rows_pool.tile([P, N], F32)
-            half_sum = stats.tile([P, HALVES], F32)
-            for h in range(HALVES):
-                nc.scalar.activation(
-                    out=e[:, half_cols[h]],
-                    in_=live["score", i, h][:],
-                    func=ACT.Exp,
-                    bias=live["neg_max", i][:],
-                    scale=1.0,
-                    accum_out=half_sum[:, h : h + 1],
-                )
-            live["e", i] = e
-            live["half_sum", i] = half_sum
-
-        def sum_of_halves(i):
             total = stats.tile([P, 1], F32)
-            nc.vector.tensor_reduce(out=total[:], in_=live["half_sum", i][:], axis=AXIS.X, op=ALU.add)
+            nc.scalar.activation(
+                out=live["row", i][:],
+                in_=live["row", i][:],
+                func=ACT.Exp,
+                bias=live["neg_max", i][:],
+                scale=-1.0,
+                accum_out=total[:],
+            )
             live["total", i] = total
 
         def normalise(i):
             inverse = stats.tile([P, 1], F32)
             nc.vector.reciprocal(out=inverse[:], in_=live["total", i][:])
-            e = live["e", i]
+            row = live["row", i]
             for h in range(HALVES):
                 nc.gpsimd.tensor_scalar(
-                    out=e[:, half_cols[h]],
-                    in0=e[:, half_cols[h]],
+                    out=row[:, half_cols[h]],
+                    in0=row[:, half_cols[h]],
                     scalar1=inverse[:],
                     scalar2=0.0,
                     op0=ALU.mult,
@@ -188,33 +193,34 @@ def tile_featuremaptransformer_pb_kernel(tc, q_ir, irSegF, Wk_dr, bk_dr, out):
                 )
 
         def flip(i):
-            e = live["e", i]
+            row = live["row", i]
             for h in range(HALVES):
-                flipped = psum.tile([P, N_TILES_PER_BANK, P], F32, tag="work")
+                flipped = flip_banks.tile([P, N_TILES_PER_BANK, P], F32, tag="flip")
                 for j in range(N_TILES_PER_BANK):
                     n_tile = h * N_TILES_PER_BANK + j
-                    nc.tensor.transpose(flipped[:, j, :], e[:, n_tile * P : (n_tile + 1) * P], identity[:])
+                    nc.tensor.transpose(flipped[:, j, :], row[:, n_tile * P : (n_tile + 1) * P], identity[:])
                 live["flipped", i, h] = flipped
 
         def store(i):
             for h in range(HALVES):
-                staged = rows_pool.tile([P, N_TILES_PER_BANK, P], F32)
-                nc.scalar.copy(out=staged[:], in_=live["flipped", i, h][:])
+                staged = staging.tile([P, N_TILES_PER_BANK, P], F32)
+                if h == 1 and i >= FIRST_SHARED_TILE:
+                    nc.vector.tensor_copy(out=staged[:], in_=live["flipped", i, h][:])
+                else:
+                    nc.scalar.copy(out=staged[:], in_=live["flipped", i, h][:])
                 n_tiles = slice(h * N_TILES_PER_BANK, (h + 1) * N_TILES_PER_BANK)
                 nc.sync.dma_start(out=out_dram[:, n_tiles, m_cols(i)], in_=staged[:])
 
         regroup(nc.vector.tensor_copy, seg_grouped[:, half_cols[0], :], seg_rows[:, :, half_cols[0]])
         regroup(nc.scalar.copy, q_grouped[:, half_cols[0], :], q_rows[:, :, half_cols[0]])
         nc.vector.quantize_mx(out=w_codes[:].bitcast(FP8X4), scales=w_scales[:], in_=w_grouped[:])
+        quantise_seg(0)
         project_keys(0)
+        project_keys(1)
         regroup(nc.vector.tensor_copy, q_grouped[:, half_cols[1], :], q_rows[:, :, half_cols[1]])
         regroup(nc.scalar.copy, seg_grouped[:, half_cols[1], :], seg_rows[:, :, half_cols[1]])
         for h in range(HALVES):
-            nc.vector.quantize_mx(
-                out=q_codes[:, half_cols[h]].bitcast(FP8X4),
-                scales=q_scales[:, half_cols[h]],
-                in_=q_grouped[:, half_cols[h], :].rearrange("p n j -> p (n j)"),
-            )
+            quantise(q_codes, q_scales, q_grouped, half_cols[h])
 
         def at(stage, i):
             if 0 <= i < M_TILES:
@@ -223,11 +229,11 @@ def tile_featuremaptransformer_pb_kernel(tc, q_ir, irSegF, Wk_dr, bk_dr, out):
         for s in range(-2, M_TILES + 1):
             at(flip, s - 1)
             at(add_bias, s + 2)
-            at(project_keys, s + 3)
-            at(max_of_halves, s + 1)
+            at(evacuate, s + 1)
             at(exponentials, s)
-            at(sum_of_halves, s)
             at(score, s + 2)
+            at(quantise_seg, s + 5)
+            at(project_keys, s + 4)
             at(negated_max, s + 1)
             at(normalise, s)
             at(store, s - 1)

@@ -47,18 +47,18 @@ def tile_featuremaptransformer_pb_kernel(tc, q_ir, irSegF, Wk_dr, bk_dr, out):
         flip_banks = ctx.enter_context(tc.psum_pool(name="flip_banks", bufs=2))
 
         w_rows = keep.tile([P, PACK * C], BF16)
-        seg_rows = keep.tile([P, PACK, N], BF16)
-        q_rows = keep.tile([P, PACK, N], BF16)
         bias = keep.tile([P, PACK], BF16)
+        seg_rows = [keep.tile([P, PACK, BANK], BF16, name="seg_rows%d" % h) for h in range(HALVES)]
+        q_rows = [keep.tile([P, PACK, BANK], BF16, name="q_rows%d" % h) for h in range(HALVES)]
         seg_dram = irSegF[0].rearrange("(p j) h w -> p j (h w)", j=PACK)
         q_dram = q_ir[0].rearrange("(p j) n -> p j n", j=PACK)
         half_cols = [slice(h * BANK, (h + 1) * BANK) for h in range(HALVES)]
         nc.sync.dma_start(out=w_rows[:], in_=Wk_dr.rearrange("(p t) c -> p (t c)", t=PACK))
         nc.scalar.dma_start(out=bias[:], in_=bk_dr.rearrange("(p t) -> p t", t=PACK))
-        nc.sync.dma_start(out=seg_rows[:, :, half_cols[0]], in_=seg_dram[:, :, half_cols[0]])
+        nc.sync.dma_start(out=seg_rows[0][:], in_=seg_dram[:, :, half_cols[0]])
         for h in range(HALVES):
-            nc.sync.dma_start(out=q_rows[:, :, half_cols[h]], in_=q_dram[:, :, half_cols[h]])
-        nc.sync.dma_start(out=seg_rows[:, :, half_cols[1]], in_=seg_dram[:, :, half_cols[1]])
+            nc.sync.dma_start(out=q_rows[h][:], in_=q_dram[:, :, half_cols[h]])
+        nc.sync.dma_start(out=seg_rows[1][:], in_=seg_dram[:, :, half_cols[1]])
 
         identity = keep.tile([P, P], F32)
         masks.make_identity(nc, identity[:])
@@ -211,14 +211,14 @@ def tile_featuremaptransformer_pb_kernel(tc, q_ir, irSegF, Wk_dr, bk_dr, out):
                 n_tiles = slice(h * N_TILES_PER_BANK, (h + 1) * N_TILES_PER_BANK)
                 nc.sync.dma_start(out=out_dram[:, n_tiles, m_cols(i)], in_=staged[:])
 
-        regroup(nc.vector.tensor_copy, seg_grouped[:, half_cols[0], :], seg_rows[:, :, half_cols[0]])
-        regroup(nc.scalar.copy, q_grouped[:, half_cols[0], :], q_rows[:, :, half_cols[0]])
+        regroup(nc.vector.tensor_copy, seg_grouped[:, half_cols[0], :], seg_rows[0][:])
+        regroup(nc.scalar.copy, q_grouped[:, half_cols[0], :], q_rows[0][:])
         nc.vector.quantize_mx(out=w_codes[:].bitcast(FP8X4), scales=w_scales[:], in_=w_grouped[:])
         quantise_seg(0)
         project_keys(0)
         project_keys(1)
-        regroup(nc.vector.tensor_copy, q_grouped[:, half_cols[1], :], q_rows[:, :, half_cols[1]])
-        regroup(nc.scalar.copy, seg_grouped[:, half_cols[1], :], seg_rows[:, :, half_cols[1]])
+        regroup(nc.vector.tensor_copy, q_grouped[:, half_cols[1], :], q_rows[1][:])
+        regroup(nc.scalar.copy, seg_grouped[:, half_cols[1], :], seg_rows[1][:])
         for h in range(HALVES):
             quantise(q_codes, q_scales, q_grouped, half_cols[h])
 

@@ -10,7 +10,6 @@ U8 = mybir.dt.uint8
 FP8X4 = mybir.dt.float8_e4m3fn_x4
 ALU = mybir.AluOpType
 ACT = mybir.ActivationFunctionType
-AXIS = mybir.AxisListType
 
 P = 128
 PACK = 4
@@ -19,10 +18,13 @@ N = 1024
 BANK = 512
 HALVES = N // BANK
 M_TILES = N // P
-TILES_PER_HALF = M_TILES // HALVES
 N_TILES_PER_BANK = BANK // P
-FIRST_SHARED_TILE = 4
 RUN = 4
+W_PARTS = 2
+W_PART_ROWS = PACK // W_PARTS
+SEG_PIECES = ((0, 256), (256, 512), (512, 1024))
+Q_VECTOR_COLS = (320, 128)
+LAST_LOOP_COPY = 3
 
 FLOPS = 2 * C * C * N + 2 * N * N * C
 
@@ -39,26 +41,29 @@ def tile_featuremaptransformer_pb_kernel(tc, q_ir, irSegF, Wk_dr, bk_dr, out):
     with ExitStack() as ctx:
         ctx.enter_context(tc.manual_schedule())
         keep = ctx.enter_context(tc.tile_pool(name="keep", bufs=1))
-        stats = ctx.enter_context(tc.tile_pool(name="stats", bufs=4))
-        rows_pool = ctx.enter_context(tc.tile_pool(name="rows", bufs=4))
-        staging = ctx.enter_context(tc.tile_pool(name="staging", bufs=6))
+        stats = ctx.enter_context(tc.tile_pool(name="stats", bufs=M_TILES))
+        rows_pool = ctx.enter_context(tc.tile_pool(name="rows", bufs=M_TILES))
+        staging = ctx.enter_context(tc.tile_pool(name="staging", bufs=8))
         score_banks = ctx.enter_context(tc.psum_pool(name="score_banks", bufs=4))
         key_banks = ctx.enter_context(tc.psum_pool(name="key_banks", bufs=2))
         flip_banks = ctx.enter_context(tc.psum_pool(name="flip_banks", bufs=2))
 
-        w_rows = keep.tile([P, PACK * C], BF16)
+        w_rows = [keep.tile([P, W_PART_ROWS * C], BF16, name="w_rows%d" % b) for b in range(W_PARTS)]
         bias = keep.tile([P, PACK], BF16)
-        seg_rows = [keep.tile([P, PACK, BANK], BF16, name="seg_rows%d" % h) for h in range(HALVES)]
+        seg_rows = [keep.tile([P, PACK, b - a], BF16, name="seg_rows%d" % k) for k, (a, b) in enumerate(SEG_PIECES)]
         q_rows = [keep.tile([P, PACK, BANK], BF16, name="q_rows%d" % h) for h in range(HALVES)]
+        w_dram = Wk_dr.rearrange("(p t) c -> p (t c)", t=PACK)
         seg_dram = irSegF[0].rearrange("(p j) h w -> p j (h w)", j=PACK)
         q_dram = q_ir[0].rearrange("(p j) n -> p j n", j=PACK)
         half_cols = [slice(h * BANK, (h + 1) * BANK) for h in range(HALVES)]
-        nc.sync.dma_start(out=w_rows[:], in_=Wk_dr.rearrange("(p t) c -> p (t c)", t=PACK))
         nc.scalar.dma_start(out=bias[:], in_=bk_dr.rearrange("(p t) -> p t", t=PACK))
-        nc.sync.dma_start(out=seg_rows[0][:], in_=seg_dram[:, :, half_cols[0]])
+        for b in range(W_PARTS):
+            nc.sync.dma_start(out=w_rows[b][:], in_=w_dram[:, b * W_PART_ROWS * C : (b + 1) * W_PART_ROWS * C])
+        nc.sync.dma_start(out=seg_rows[0][:], in_=seg_dram[:, :, SEG_PIECES[0][0] : SEG_PIECES[0][1]])
         for h in range(HALVES):
             nc.sync.dma_start(out=q_rows[h][:], in_=q_dram[:, :, half_cols[h]])
-        nc.sync.dma_start(out=seg_rows[1][:], in_=seg_dram[:, :, half_cols[1]])
+        for k in range(1, len(SEG_PIECES)):
+            nc.sync.dma_start(out=seg_rows[k][:], in_=seg_dram[:, :, SEG_PIECES[k][0] : SEG_PIECES[k][1]])
 
         identity = keep.tile([P, P], F32)
         masks.make_identity(nc, identity[:])
@@ -67,21 +72,10 @@ def tile_featuremaptransformer_pb_kernel(tc, q_ir, irSegF, Wk_dr, bk_dr, out):
         nc.vector.memset(warm[:], 0.0)
         nc.scalar.activation(out=warm[:], in_=warm[:], func=ACT.Exp)
 
-        w_words = w_rows[:].bitcast(F32).rearrange("o (t p u) -> o t u p", t=PACK, u=2)
         w_grouped = keep.tile([P, PACK * P * PACK], BF16, align_bytes=64)
         w_grouped_words = w_grouped[:].bitcast(F32).rearrange("p (t o u) -> p t o u", t=PACK, u=2)
         w_codes = keep.tile([P, PACK * P], U32, align_bytes=64)
         w_scales = keep.tile([P, PACK * P], U8, align_bytes=64)
-        for b in range(2):
-            w_t = flip_banks.tile([P, 2, 2, P], F32, tag="flip")
-            for t in range(2):
-                for u in range(2):
-                    nc.tensor.transpose(w_t[:, t, u, :], w_words[:, 2 * b + t, u, :], identity[:])
-            nc.scalar.copy(
-                out=w_grouped_words[:, 2 * b : 2 * b + 2, :, :],
-                in_=w_t[:].rearrange("p t u o -> p t o u"),
-            )
-
         q_grouped = keep.tile([P, N, PACK], BF16, align_bytes=64)
         q_codes = keep.tile([P, N], U32, align_bytes=64)
         q_scales = keep.tile([P, N], U8, align_bytes=64)
@@ -97,6 +91,22 @@ def tile_featuremaptransformer_pb_kernel(tc, q_ir, irSegF, Wk_dr, bk_dr, out):
         def m_cols(i):
             return slice(i * P, (i + 1) * P)
 
+        def flip_w(b):
+            w_words = w_rows[b][:].bitcast(F32).rearrange("o (t p u) -> o t u p", t=W_PART_ROWS, u=2)
+            w_t = flip_banks.tile([P, W_PART_ROWS, 2, P], F32, tag="flip")
+            for t in range(W_PART_ROWS):
+                for u in range(2):
+                    nc.tensor.transpose(w_t[:, t, u, :], w_words[:, t, u, :], identity[:])
+            nc.scalar.copy(
+                out=w_grouped_words[:, b * W_PART_ROWS : (b + 1) * W_PART_ROWS, :, :],
+                in_=w_t[:].rearrange("p t u o -> p t o u"),
+            )
+
+        def quantise_w(b):
+            words = slice(b * W_PART_ROWS * P, (b + 1) * W_PART_ROWS * P)
+            values = slice(b * W_PART_ROWS * P * PACK, (b + 1) * W_PART_ROWS * P * PACK)
+            nc.vector.quantize_mx(out=w_codes[:, words].bitcast(FP8X4), scales=w_scales[:, words], in_=w_grouped[:, values])
+
         def quantise(codes, scales, grouped, cols):
             nc.vector.quantize_mx(
                 out=codes[:, cols].bitcast(FP8X4),
@@ -104,9 +114,18 @@ def tile_featuremaptransformer_pb_kernel(tc, q_ir, irSegF, Wk_dr, bk_dr, out):
                 in_=grouped[:, cols, :].rearrange("p w j -> p (w j)"),
             )
 
-        def quantise_seg(i):
-            if i % TILES_PER_HALF == 0:
-                quantise(seg_codes, seg_scales, seg_grouped, half_cols[i // TILES_PER_HALF])
+        def quantise_seg(a, b):
+            quantise(seg_codes, seg_scales, seg_grouped, slice(a, b))
+
+        def quantise_q(h):
+            quantise(q_codes, q_scales, q_grouped, half_cols[h])
+
+        def regroup_seg(copy, k, a, b):
+            first = SEG_PIECES[k][0]
+            regroup(copy, seg_grouped[:, a:b, :], seg_rows[k][:, :, a - first : b - first])
+
+        def regroup_q(copy, h, a, b):
+            regroup(copy, q_grouped[:, h * BANK + a : h * BANK + b, :], q_rows[h][:, :, a:b])
 
         def project_keys(i):
             key_bank = key_banks.tile([P, PACK, P], F32, tag="key")
@@ -130,41 +149,42 @@ def tile_featuremaptransformer_pb_kernel(tc, q_ir, irSegF, Wk_dr, bk_dr, out):
                 op=ALU.add,
             )
 
-        def score(i):
+        def quantise_key(i):
             quantise(key_codes, key_scales, key_grouped, m_cols(i))
-            for h in range(HALVES):
-                score_bank = score_banks.tile([P, BANK], F32, tag="score")
-                nc.tensor.matmul_mx(
-                    out=score_bank[:],
-                    lhsT=key_codes[:, m_cols(i)].bitcast(FP8X4),
-                    lhsT_scale=key_scales[:, m_cols(i)],
-                    rhs=q_codes[:, half_cols[h]].bitcast(FP8X4),
-                    rhs_scale=q_scales[:, half_cols[h]],
-                    start=True,
-                    stop=True,
-                )
-                live["score", i, h] = score_bank
 
-        def evacuate(i):
-            row = rows_pool.tile([P, N], F32)
-            half_min = stats.tile([P, HALVES], F32)
-            for h in range(HALVES):
-                nc.vector.tensor_scalar(
-                    out=row[:, half_cols[h]],
-                    in0=live["score", i, h][:],
-                    scalar1=-1.0,
-                    scalar2=None,
-                    op0=ALU.mult,
-                    op1=ALU.min,
-                    accum_out=half_min[:, h : h + 1],
-                )
-            live["row", i] = row
-            live["half_min", i] = half_min
+        def score_half(i, h):
+            score_bank = score_banks.tile([P, BANK], F32, tag="score")
+            nc.tensor.matmul_mx(
+                out=score_bank[:],
+                lhsT=key_codes[:, m_cols(i)].bitcast(FP8X4),
+                lhsT_scale=key_scales[:, m_cols(i)],
+                rhs=q_codes[:, half_cols[h]].bitcast(FP8X4),
+                rhs_scale=q_scales[:, half_cols[h]],
+                start=True,
+                stop=True,
+            )
+            live["score", i, h] = score_bank
 
-        def negated_max(i):
-            neg_max = stats.tile([P, 1], F32)
-            nc.vector.tensor_reduce(out=neg_max[:], in_=live["half_min", i][:], axis=AXIS.X, op=ALU.min)
-            live["neg_max", i] = neg_max
+        def score(i):
+            for h in range(HALVES):
+                score_half(i, h)
+
+        def evacuate(i, h):
+            if h == 0:
+                row = rows_pool.tile([P, N], F32)
+                mins = stats.tile([P, HALVES], F32)
+                live["row", i] = row
+                live["mins", i] = mins
+            mins = live["mins", i]
+            nc.vector.tensor_scalar(
+                out=live["row", i][:, half_cols[h]],
+                in0=live["score", i, h][:],
+                scalar1=-1.0,
+                scalar2=None if h == 0 else mins[:, h - 1 : h],
+                op0=ALU.mult,
+                op1=ALU.min,
+                accum_out=mins[:, h : h + 1],
+            )
 
         def exponentials(i):
             total = stats.tile([P, 1], F32)
@@ -172,68 +192,121 @@ def tile_featuremaptransformer_pb_kernel(tc, q_ir, irSegF, Wk_dr, bk_dr, out):
                 out=live["row", i][:],
                 in_=live["row", i][:],
                 func=ACT.Exp,
-                bias=live["neg_max", i][:],
+                bias=live["mins", i][:, HALVES - 1 : HALVES],
                 scale=-1.0,
                 accum_out=total[:],
             )
             live["total", i] = total
 
-        def normalise(i):
+        def invert_sum(i):
             inverse = stats.tile([P, 1], F32)
             nc.vector.reciprocal(out=inverse[:], in_=live["total", i][:])
+            live["inverse", i] = inverse
+
+        def scale_on_gpsimd(i):
             row = live["row", i]
             for h in range(HALVES):
                 nc.gpsimd.tensor_scalar(
                     out=row[:, half_cols[h]],
                     in0=row[:, half_cols[h]],
-                    scalar1=inverse[:],
+                    scalar1=live["inverse", i][:],
                     scalar2=0.0,
                     op0=ALU.mult,
                     op1=ALU.add,
                 )
 
-        def flip(i):
+        def scale_on_vector(i):
             row = live["row", i]
             for h in range(HALVES):
-                flipped = flip_banks.tile([P, N_TILES_PER_BANK, P], F32, tag="flip")
+                nc.vector.tensor_scalar(
+                    out=row[:, half_cols[h]],
+                    in0=row[:, half_cols[h]],
+                    scalar1=live["inverse", i][:],
+                    scalar2=None,
+                    op0=ALU.mult,
+                )
+
+        def flip(i, banks, tag):
+            row = live["row", i]
+            for h in range(HALVES):
+                flipped = banks.tile([P, N_TILES_PER_BANK, P], F32, tag=tag)
                 for j in range(N_TILES_PER_BANK):
                     n_tile = h * N_TILES_PER_BANK + j
                     nc.tensor.transpose(flipped[:, j, :], row[:, n_tile * P : (n_tile + 1) * P], identity[:])
                 live["flipped", i, h] = flipped
 
-        def store(i):
-            for h in range(HALVES):
-                staged = staging.tile([P, N_TILES_PER_BANK, P], F32)
-                if h == 1 and i >= FIRST_SHARED_TILE:
-                    nc.vector.tensor_copy(out=staged[:], in_=live["flipped", i, h][:])
-                else:
-                    nc.scalar.copy(out=staged[:], in_=live["flipped", i, h][:])
-                n_tiles = slice(h * N_TILES_PER_BANK, (h + 1) * N_TILES_PER_BANK)
-                nc.sync.dma_start(out=out_dram[:, n_tiles, m_cols(i)], in_=staged[:])
+        def copy_out(copy, i, h):
+            staged = staging.tile([P, N_TILES_PER_BANK, P], F32)
+            copy(out=staged[:], in_=live["flipped", i, h][:])
+            n_tiles = slice(h * N_TILES_PER_BANK, (h + 1) * N_TILES_PER_BANK)
+            nc.sync.dma_start(out=out_dram[:, n_tiles, m_cols(i)], in_=staged[:])
 
-        regroup(nc.vector.tensor_copy, seg_grouped[:, half_cols[0], :], seg_rows[0][:])
-        regroup(nc.scalar.copy, q_grouped[:, half_cols[0], :], q_rows[0][:])
-        nc.vector.quantize_mx(out=w_codes[:].bitcast(FP8X4), scales=w_scales[:], in_=w_grouped[:])
-        quantise_seg(0)
+        on_vector = nc.vector.tensor_copy
+        on_scalar = nc.scalar.copy
+
+        for b in range(W_PARTS):
+            flip_w(b)
+        regroup_seg(on_vector, 0, 0, 256)
+        quantise_w(0)
+        quantise_seg(0, 256)
+        regroup_q(on_scalar, 0, Q_VECTOR_COLS[0], BANK)
+        regroup_q(on_vector, 0, 0, Q_VECTOR_COLS[0])
+        quantise_w(1)
         project_keys(0)
         project_keys(1)
-        regroup(nc.vector.tensor_copy, q_grouped[:, half_cols[1], :], q_rows[1][:])
-        regroup(nc.scalar.copy, seg_grouped[:, half_cols[1], :], seg_rows[1][:])
-        for h in range(HALVES):
-            quantise(q_codes, q_scales, q_grouped, half_cols[h])
+        regroup_q(on_scalar, 1, Q_VECTOR_COLS[1], BANK)
+        quantise_q(0)
+        regroup_q(on_vector, 1, 0, Q_VECTOR_COLS[1])
+        add_bias(0)
+        regroup_seg(on_scalar, 1, 256, 512)
+        quantise_key(0)
+        score_half(0, 0)
+        add_bias(1)
+        quantise_q(1)
+        score_half(0, 1)
+        quantise_seg(256, 512)
+        regroup_seg(on_scalar, 2, 512, 768)
 
-        def at(stage, i):
+        def at(stage, i, *more):
             if 0 <= i < M_TILES:
-                stage(i)
+                stage(i, *more)
 
-        for s in range(-2, M_TILES + 1):
-            at(flip, s - 1)
-            at(add_bias, s + 2)
-            at(evacuate, s + 1)
+        for s in range(-1, M_TILES - 1):
+            at(flip, s - 2, flip_banks, "flip")
+            if s >= 0:
+                at(add_bias, s + 2)
+            at(evacuate, s + 1, 0)
+            at(quantise_key, s + 2)
+            at(invert_sum, s - 1)
+            at(scale_on_gpsimd, s - 1)
+            at(evacuate, s + 1, 1)
             at(exponentials, s)
+            if s == -1:
+                quantise_seg(512, 768)
+            if s == 0:
+                regroup_seg(on_scalar, 2, 768, 1024)
+            if s == 1:
+                quantise_seg(768, 1024)
+            at(project_keys, s + 3)
             at(score, s + 2)
-            at(quantise_seg, s + 5)
-            at(project_keys, s + 4)
-            at(negated_max, s + 1)
-            at(normalise, s)
-            at(store, s - 1)
+            if 0 <= s - 2 <= LAST_LOOP_COPY:
+                for h in range(HALVES):
+                    copy_out(on_scalar, s - 2, h)
+
+        last = M_TILES - 1
+        exponentials(last)
+        for h in range(HALVES):
+            copy_out(on_vector, last - 3, h)
+        flip(last - 2, flip_banks, "flip")
+        invert_sum(last - 1)
+        scale_on_vector(last - 1)
+        flip(last - 1, score_banks, "score")
+        invert_sum(last)
+        scale_on_vector(last)
+        for h in range(HALVES):
+            copy_out(on_scalar, last - 2, h)
+        flip(last, score_banks, "score")
+        copy_out(on_scalar, last - 1, 0)
+        copy_out(on_vector, last - 1, 1)
+        copy_out(on_vector, last, 0)
+        copy_out(on_scalar, last, 1)

@@ -277,6 +277,8 @@ def tile_featuremaptransformer_pb_kernel(tc, q_ir, irSegF, Wk_dr, bk_dr, out):
                 at(add_bias, s + 2)
             at(evacuate, s + 1, 0)
             at(quantise_key, s + 2)
+            if s == 1:
+                quantise_seg(768, 1024)
             at(invert_sum, s - 1)
             at(scale_on_gpsimd, s - 1)
             at(evacuate, s + 1, 1)
@@ -285,8 +287,6 @@ def tile_featuremaptransformer_pb_kernel(tc, q_ir, irSegF, Wk_dr, bk_dr, out):
                 quantise_seg(512, 768)
             if s == 0:
                 regroup_seg(on_scalar, 2, 768, 1024)
-            if s == 1:
-                quantise_seg(768, 1024)
             at(project_keys, s + 3)
             at(score, s + 2)
             if 0 <= s - 2 <= LAST_LOOP_COPY:

@@ -24,7 +24,8 @@ W_PARTS = 2
 W_PART_ROWS = PACK // W_PARTS
 SEG_PIECES = ((0, 256), (256, 512), (512, 1024))
 Q_VECTOR_COLS = (320, 128)
-LAST_LOOP_COPY = 3
+LAST_LOOP_COPY = 4
+LAST_GPSIMD_TILE = 5
 
 FLOPS = 2 * C * C * N + 2 * N * N * C
 
@@ -271,42 +272,40 @@ def tile_featuremaptransformer_pb_kernel(tc, q_ir, irSegF, Wk_dr, bk_dr, out):
             if 0 <= i < M_TILES:
                 stage(i, *more)
 
-        for s in range(-1, M_TILES - 1):
-            at(flip, s - 2, flip_banks, "flip")
+        last = M_TILES - 1
+        for s in range(-1, last):
+            at(flip, s - 1, flip_banks, "flip")
             if s >= 0:
                 at(add_bias, s + 2)
             at(evacuate, s + 1, 0)
             at(quantise_key, s + 2)
             if s == 1:
                 quantise_seg(768, 1024)
-            at(invert_sum, s - 1)
-            at(scale_on_gpsimd, s - 1)
-            at(evacuate, s + 1, 1)
             at(exponentials, s)
+            if s <= LAST_GPSIMD_TILE:
+                at(invert_sum, s)
+                at(scale_on_gpsimd, s)
+            at(evacuate, s + 1, 1)
             if s == -1:
                 quantise_seg(512, 768)
             if s == 0:
                 regroup_seg(on_scalar, 2, 768, 1024)
             at(project_keys, s + 3)
             at(score, s + 2)
-            if 0 <= s - 2 <= LAST_LOOP_COPY:
+            if 0 <= s - 1 <= LAST_LOOP_COPY:
                 for h in range(HALVES):
-                    copy_out(on_scalar, s - 2, h)
+                    copy_out(on_scalar, s - 1, h)
 
-        last = M_TILES - 1
         exponentials(last)
-        for h in range(HALVES):
-            copy_out(on_vector, last - 3, h)
-        flip(last - 2, flip_banks, "flip")
+        copy_out(on_vector, last - 2, 0)
         invert_sum(last - 1)
         scale_on_vector(last - 1)
         flip(last - 1, score_banks, "score")
+        copy_out(on_vector, last - 2, 1)
         invert_sum(last)
         scale_on_vector(last)
+        flip(last, flip_banks, "flip")
         for h in range(HALVES):
-            copy_out(on_scalar, last - 2, h)
-        flip(last, score_banks, "score")
-        copy_out(on_scalar, last - 1, 0)
-        copy_out(on_vector, last - 1, 1)
+            copy_out(on_scalar, last - 1, h)
         copy_out(on_vector, last, 0)
         copy_out(on_scalar, last, 1)

@@ -23,7 +23,7 @@ RUN = 4
 W_PARTS = 2
 W_PART_ROWS = PACK // W_PARTS
 SEG_PIECES = ((0, 256), (256, 512), (512, 1024))
-Q_VECTOR_COLS = (320, 128)
+Q_VECTOR_COLS = (320, 192)
 LAST_LOOP_COPY = 4
 LAST_GPSIMD_TILE = 5
 
@@ -260,9 +260,9 @@ def tile_featuremaptransformer_pb_kernel(tc, q_ir, irSegF, Wk_dr, bk_dr, out):
         regroup_q(on_vector, 1, 0, Q_VECTOR_COLS[1])
         add_bias(0)
         regroup_seg(on_scalar, 1, 256, 512)
+        add_bias(1)
         quantise_key(0)
         score_half(0, 0)
-        add_bias(1)
         quantise_q(1)
         score_half(0, 1)
         quantise_seg(256, 512)
@@ -301,11 +301,11 @@ def tile_featuremaptransformer_pb_kernel(tc, q_ir, irSegF, Wk_dr, bk_dr, out):
         invert_sum(last - 1)
         scale_on_vector(last - 1)
         flip(last - 1, score_banks, "score")
-        copy_out(on_vector, last - 2, 1)
         invert_sum(last)
         scale_on_vector(last)
-        flip(last, flip_banks, "flip")
-        for h in range(HALVES):
-            copy_out(on_scalar, last - 1, h)
+        copy_out(on_scalar, last - 2, 1)
+        flip(last, score_banks, "score")
+        copy_out(on_scalar, last - 1, 0)
+        copy_out(on_vector, last - 1, 1)
         copy_out(on_vector, last, 0)
         copy_out(on_scalar, last, 1)

@@ -24,6 +24,7 @@ W_PARTS = 2
 W_PART_ROWS = PACK // W_PARTS
 SEG_PIECES = ((0, 256), (256, 512), (512, 1024))
 Q_VECTOR_COLS = (320, 192)
+STORE_GROUPS = (2, 2, 1, 1, 1, 1)
 LAST_LOOP_COPY = 4
 LAST_GPSIMD_TILE = 5
 
@@ -236,11 +237,24 @@ def tile_featuremaptransformer_pb_kernel(tc, q_ir, irSegF, Wk_dr, bk_dr, out):
                     nc.tensor.transpose(flipped[:, j, :], row[:, n_tile * P : (n_tile + 1) * P], identity[:])
                 live["flipped", i, h] = flipped
 
+        group_of = {}
+        first = 0
+        for size in STORE_GROUPS:
+            for i in range(first, first + size):
+                group_of[i] = (first, size)
+            first += size
+
         def copy_out(copy, i, h):
-            staged = staging.tile([P, N_TILES_PER_BANK, P], F32)
-            copy(out=staged[:], in_=live["flipped", i, h][:])
-            n_tiles = slice(h * N_TILES_PER_BANK, (h + 1) * N_TILES_PER_BANK)
-            nc.sync.dma_start(out=out_dram[:, n_tiles, m_cols(i)], in_=staged[:])
+            first_tile, size = group_of[i]
+            if i == first_tile:
+                staged = staging.tile([P, N_TILES_PER_BANK, size * P], F32, name="staged%d" % size)
+                live["staged", first_tile, h] = staged
+            staged = live["staged", first_tile, h]
+            place = i - first_tile
+            copy(out=staged[:, :, place * P : (place + 1) * P], in_=live["flipped", i, h][:])
+            if place == size - 1:
+                n_tiles = slice(h * N_TILES_PER_BANK, (h + 1) * N_TILES_PER_BANK)
+                nc.sync.dma_start(out=out_dram[:, n_tiles, first_tile * P : (first_tile + size) * P], in_=staged[:])
 
         on_vector = nc.vector.tensor_copy
         on_scalar = nc.scalar.copy

@@ -228,9 +228,9 @@ def tile_featuremaptransformer_pb_kernel(tc, q_ir, irSegF, Wk_dr, bk_dr, out):
                     op0=ALU.mult,
                 )
 
-        def flip(i, banks, tag):
+        def flip(i, banks, tag, halves=range(HALVES)):
             row = live["row", i]
-            for h in range(HALVES):
+            for h in halves:
                 flipped = banks.tile([P, N_TILES_PER_BANK, P], F32, tag=tag)
                 for j in range(N_TILES_PER_BANK):
                     n_tile = h * N_TILES_PER_BANK + j
@@ -244,17 +244,23 @@ def tile_featuremaptransformer_pb_kernel(tc, q_ir, irSegF, Wk_dr, bk_dr, out):
                 group_of[i] = (first, size)
             first += size
 
-        def copy_out(copy, i, h):
+        def copy_out(copy, i, h, a=0, b=N_TILES_PER_BANK):
             first_tile, size = group_of[i]
-            if i == first_tile:
+            if ("staged", first_tile, h) not in live:
                 staged = staging.tile([P, N_TILES_PER_BANK, size * P], F32, name="staged%d" % size)
                 live["staged", first_tile, h] = staged
             staged = live["staged", first_tile, h]
             place = i - first_tile
-            copy(out=staged[:, :, place * P : (place + 1) * P], in_=live["flipped", i, h][:])
-            if place == size - 1:
+            copy(out=staged[:, a:b, place * P : (place + 1) * P], in_=live["flipped", i, h][:, a:b, :])
+
+        def store(i, h):
+            first_tile, size = group_of[i]
+            if i == first_tile + size - 1:
                 n_tiles = slice(h * N_TILES_PER_BANK, (h + 1) * N_TILES_PER_BANK)
-                nc.sync.dma_start(out=out_dram[:, n_tiles, first_tile * P : (first_tile + size) * P], in_=staged[:])
+                nc.sync.dma_start(
+                    out=out_dram[:, n_tiles, first_tile * P : (first_tile + size) * P],
+                    in_=live["staged", first_tile, h][:],
+                )
 
         on_vector = nc.vector.tensor_copy
         on_scalar = nc.scalar.copy
@@ -288,7 +294,10 @@ def tile_featuremaptransformer_pb_kernel(tc, q_ir, irSegF, Wk_dr, bk_dr, out):
 
         last = M_TILES - 1
         for s in range(-1, last):
-            at(flip, s - 1, flip_banks, "flip")
+            if s >= 2:
+                flip(s - 2, flip_banks, "flip", (1,))
+            if s >= 1:
+                flip(s - 1, flip_banks, "flip", (0,))
             if s >= 0:
                 at(add_bias, s + 2)
             at(evacuate, s + 1, 0)
@@ -300,26 +309,36 @@ def tile_featuremaptransformer_pb_kernel(tc, q_ir, irSegF, Wk_dr, bk_dr, out):
                 at(invert_sum, s)
                 at(scale_on_gpsimd, s)
             at(evacuate, s + 1, 1)
+            at(project_keys, s + 3)
+            at(score, s + 2)
             if s == -1:
                 quantise_seg(512, 768)
             if s == 0:
                 regroup_seg(on_scalar, 2, 768, 1024)
-            at(project_keys, s + 3)
-            at(score, s + 2)
-            if 0 <= s - 1 <= LAST_LOOP_COPY:
-                for h in range(HALVES):
-                    copy_out(on_scalar, s - 1, h)
+            if 2 <= s < last:
+                copy_out(on_scalar, s - 2, 1)
+                store(s - 2, 1)
+            if 1 <= s < last - 1:
+                copy_out(on_scalar, s - 1, 0)
+                store(s - 1, 0)
 
         exponentials(last)
-        copy_out(on_vector, last - 2, 0)
+        flip(last - 2, key_banks, "key", (1,))
         invert_sum(last - 1)
+        copy_out(on_vector, last - 2, 0)
+        store(last - 2, 0)
         scale_on_vector(last - 1)
         flip(last - 1, score_banks, "score")
+        copy_out(on_scalar, last - 2, 1)
+        store(last - 2, 1)
         invert_sum(last)
         scale_on_vector(last)
-        copy_out(on_scalar, last - 2, 1)
         flip(last, score_banks, "score")
         copy_out(on_scalar, last - 1, 0)
+        store(last - 1, 0)
         copy_out(on_vector, last - 1, 1)
+        store(last - 1, 1)
         copy_out(on_vector, last, 0)
+        store(last, 0)
         copy_out(on_scalar, last, 1)
+        store(last, 1)

@@ -24,7 +24,7 @@ W_PARTS = 2
 W_PART_ROWS = PACK // W_PARTS
 SEG_PIECES = ((0, 256), (256, 512), (512, 1024))
 Q_VECTOR_COLS = (320, 192)
-STORE_GROUPS = (2, 2, 1, 1, 1, 1)
+STORE_GROUPS = (1, 1, 1, 1, 1, 1, 1, 1)
 LAST_LOOP_COPY = 4
 LAST_GPSIMD_TILE = 5
 

@@ -45,7 +45,7 @@ def tile_featuremaptransformer_pb_kernel(tc, q_ir, irSegF, Wk_dr, bk_dr, out):
         keep = ctx.enter_context(tc.tile_pool(name="keep", bufs=1))
         stats = ctx.enter_context(tc.tile_pool(name="stats", bufs=M_TILES))
         rows_pool = ctx.enter_context(tc.tile_pool(name="rows", bufs=M_TILES))
-        staging = ctx.enter_context(tc.tile_pool(name="staging", bufs=8))
+        staging = ctx.enter_context(tc.tile_pool(name="staging", bufs=16))
         score_banks = ctx.enter_context(tc.psum_pool(name="score_banks", bufs=4))
         key_banks = ctx.enter_context(tc.psum_pool(name="key_banks", bufs=2))
         flip_banks = ctx.enter_context(tc.psum_pool(name="flip_banks", bufs=2))
@@ -305,38 +305,39 @@ def tile_featuremaptransformer_pb_kernel(tc, q_ir, irSegF, Wk_dr, bk_dr, out):
             if s == 1:
                 quantise_seg(768, 1024)
             at(exponentials, s)
+            if s == last - 1:
+                copy_out(on_vector, s - 2, 1)
+                store(s - 2, 1)
             if s <= LAST_GPSIMD_TILE:
                 at(invert_sum, s)
                 at(scale_on_gpsimd, s)
             at(evacuate, s + 1, 1)
-            at(project_keys, s + 3)
-            at(score, s + 2)
             if s == -1:
                 quantise_seg(512, 768)
             if s == 0:
                 regroup_seg(on_scalar, 2, 768, 1024)
-            if 2 <= s < last:
+            at(project_keys, s + 3)
+            at(score, s + 2)
+            if 2 <= s < last - 1:
                 copy_out(on_scalar, s - 2, 1)
                 store(s - 2, 1)
-            if 1 <= s < last - 1:
+            if 1 <= s < last:
                 copy_out(on_scalar, s - 1, 0)
                 store(s - 1, 0)
 
         exponentials(last)
         flip(last - 2, key_banks, "key", (1,))
         invert_sum(last - 1)
-        copy_out(on_vector, last - 2, 0)
-        store(last - 2, 0)
         scale_on_vector(last - 1)
         flip(last - 1, score_banks, "score")
-        copy_out(on_scalar, last - 2, 1)
+        copy_out(on_vector, last - 2, 1)
         store(last - 2, 1)
+        copy_out(on_scalar, last - 1, 0)
+        store(last - 1, 0)
         invert_sum(last)
         scale_on_vector(last)
         flip(last, score_banks, "score")
-        copy_out(on_scalar, last - 1, 0)
-        store(last - 1, 0)
-        copy_out(on_vector, last - 1, 1)
+        copy_out(on_scalar, last - 1, 1)
         store(last - 1, 1)
         copy_out(on_vector, last, 0)
         store(last, 0)

@@ -90,6 +90,11 @@ def tile_featuremaptransformer_pb_kernel(tc, q_ir, irSegF, Wk_dr, bk_dr, out):
         out_dram = out[0].rearrange("(j p) m -> p j m", p=P)
         live = {}
 
+        def keep_tensor_awake(turns):
+            warm_bank = flip_banks.tile([P, P], F32, tag="flip")
+            for turn in range(turns):
+                nc.tensor.matmul(warm_bank[:], lhsT=identity[:], rhs=identity[:], start=True, stop=True)
+
         def m_cols(i):
             return slice(i * P, (i + 1) * P)
 
@@ -265,8 +270,10 @@ def tile_featuremaptransformer_pb_kernel(tc, q_ir, irSegF, Wk_dr, bk_dr, out):
         on_vector = nc.vector.tensor_copy
         on_scalar = nc.scalar.copy
 
+        keep_tensor_awake(3)
         for b in range(W_PARTS):
             flip_w(b)
+        keep_tensor_awake(3)
         regroup_seg(on_vector, 0, 0, 256)
         quantise_w(0)
         quantise_seg(0, 256)
@@ -275,6 +282,7 @@ def tile_featuremaptransformer_pb_kernel(tc, q_ir, irSegF, Wk_dr, bk_dr, out):
         quantise_w(1)
         project_keys(0)
         project_keys(1)
+        keep_tensor_awake(4)
         regroup_q(on_scalar, 1, Q_VECTOR_COLS[1], BANK)
         quantise_q(0)
         regroup_q(on_vector, 1, 0, Q_VECTOR_COLS[1])

@@ -58,12 +58,12 @@ def tile_featuremaptransformer_pb_kernel(tc, q_ir, irSegF, Wk_dr, bk_dr, out):
         seg_dram = irSegF[0].rearrange("(p j) h w -> p j (h w)", j=PACK)
         q_dram = q_ir[0].rearrange("(p j) n -> p j n", j=PACK)
         half_cols = [slice(h * BANK, (h + 1) * BANK) for h in range(HALVES)]
-        nc.scalar.dma_start(out=bias[:], in_=bk_dr.rearrange("(p t) -> p t", t=PACK))
         for b in range(W_PARTS):
             nc.sync.dma_start(out=w_rows[b][:], in_=w_dram[:, b * W_PART_ROWS * C : (b + 1) * W_PART_ROWS * C])
         nc.sync.dma_start(out=seg_rows[0][:], in_=seg_dram[:, :, SEG_PIECES[0][0] : SEG_PIECES[0][1]])
         for h in range(HALVES):
             nc.sync.dma_start(out=q_rows[h][:], in_=q_dram[:, :, half_cols[h]])
+        nc.sync.dma_start(out=bias[:], in_=bk_dr.rearrange("(p t) -> p t", t=PACK))
         for k in range(1, len(SEG_PIECES)):
             nc.sync.dma_start(out=seg_rows[k][:], in_=seg_dram[:, :, SEG_PIECES[k][0] : SEG_PIECES[k][1]])
 

from contextlib import ExitStack

import concourse.masks as masks
import concourse.mybir as mybir

BF16 = mybir.dt.bfloat16
F32 = mybir.dt.float32
U32 = mybir.dt.uint32
U8 = mybir.dt.uint8
FP8X4 = mybir.dt.float8_e4m3fn_x4
ALU = mybir.AluOpType
ACT = mybir.ActivationFunctionType

P = 128
PACK = 4
C = P * PACK
N = 1024
BANK = 512
HALVES = N // BANK
M_TILES = N // P
N_TILES_PER_BANK = BANK // P
RUN = 4
W_PARTS = 2
W_PART_ROWS = PACK // W_PARTS
SEG_PIECES = ((0, 256), (256, 512), (512, 1024))
Q_VECTOR_COLS = (320, 192)
STORE_GROUPS = (1, 1, 1, 1, 1, 1, 1, 1)
LAST_LOOP_COPY = 4
LAST_GPSIMD_TILE = 5

FLOPS = 2 * C * C * N + 2 * N * N * C


def regroup(copy, grouped, rows):
    copy(
        out=grouped.rearrange("p (c i) j -> p c j i", i=RUN),
        in_=rows.rearrange("p j (c i) -> p c j i", i=RUN),
    )


def tile_featuremaptransformer_pb_kernel(tc, q_ir, irSegF, Wk_dr, bk_dr, out):
    nc = tc.nc
    with ExitStack() as ctx:
        ctx.enter_context(tc.manual_schedule())
        keep = ctx.enter_context(tc.tile_pool(name="keep", bufs=1))
        stats = ctx.enter_context(tc.tile_pool(name="stats", bufs=M_TILES))
        rows_pool = ctx.enter_context(tc.tile_pool(name="rows", bufs=M_TILES))
        staging = ctx.enter_context(tc.tile_pool(name="staging", bufs=16))
        score_banks = ctx.enter_context(tc.psum_pool(name="score_banks", bufs=4))
        key_banks = ctx.enter_context(tc.psum_pool(name="key_banks", bufs=2))
        flip_banks = ctx.enter_context(tc.psum_pool(name="flip_banks", bufs=2))

        w_rows = [keep.tile([P, W_PART_ROWS * C], BF16, name="w_rows%d" % b) for b in range(W_PARTS)]
        bias = keep.tile([P, PACK], BF16)
        seg_rows = [keep.tile([P, PACK, b - a], BF16, name="seg_rows%d" % k) for k, (a, b) in enumerate(SEG_PIECES)]
        q_rows = [keep.tile([P, PACK, BANK], BF16, name="q_rows%d" % h) for h in range(HALVES)]
        w_dram = Wk_dr.rearrange("(p t) c -> p (t c)", t=PACK)
        seg_dram = irSegF[0].rearrange("(p j) h w -> p j (h w)", j=PACK)
        q_dram = q_ir[0].rearrange("(p j) n -> p j n", j=PACK)
        half_cols = [slice(h * BANK, (h + 1) * BANK) for h in range(HALVES)]
        for b in range(W_PARTS):
            nc.sync.dma_start(out=w_rows[b][:], in_=w_dram[:, b * W_PART_ROWS * C : (b + 1) * W_PART_ROWS * C])
        nc.sync.dma_start(out=seg_rows[0][:], in_=seg_dram[:, :, SEG_PIECES[0][0] : SEG_PIECES[0][1]])
        for h in range(HALVES):
            nc.sync.dma_start(out=q_rows[h][:], in_=q_dram[:, :, half_cols[h]])
        nc.sync.dma_start(out=bias[:], in_=bk_dr.rearrange("(p t) -> p t", t=PACK))
        for k in range(1, len(SEG_PIECES)):
            nc.sync.dma_start(out=seg_rows[k][:], in_=seg_dram[:, :, SEG_PIECES[k][0] : SEG_PIECES[k][1]])

        identity = keep.tile([P, P], F32)
        masks.make_identity(nc, identity[:])

        warm = keep.tile([P, 1], F32)
        nc.vector.memset(warm[:], 0.0)
        nc.scalar.activation(out=warm[:], in_=warm[:], func=ACT.Exp)

        w_grouped = keep.tile([P, PACK * P * PACK], BF16, align_bytes=64)
        w_grouped_words = w_grouped[:].bitcast(F32).rearrange("p (t o u) -> p t o u", t=PACK, u=2)
        w_codes = keep.tile([P, PACK * P], U32, align_bytes=64)
        w_scales = keep.tile([P, PACK * P], U8, align_bytes=64)
        q_grouped = keep.tile([P, N, PACK], BF16, align_bytes=64)
        q_codes = keep.tile([P, N], U32, align_bytes=64)
        q_scales = keep.tile([P, N], U8, align_bytes=64)
        seg_grouped = keep.tile([P, N, PACK], BF16, align_bytes=64)
        seg_codes = keep.tile([P, N], U32, align_bytes=64)
        seg_scales = keep.tile([P, N], U8, align_bytes=64)
        key_grouped = keep.tile([P, N, PACK], BF16, align_bytes=64)
        key_codes = keep.tile([P, N], U32, align_bytes=64)
        key_scales = keep.tile([P, N], U8, align_bytes=64)
        out_dram = out[0].rearrange("(j p) m -> p j m", p=P)
        live = {}

        def keep_tensor_awake(turns):
            warm_bank = flip_banks.tile([P, P], F32, tag="flip")
            for turn in range(turns):
                nc.tensor.matmul(warm_bank[:], lhsT=identity[:], rhs=identity[:], start=True, stop=True)

        def m_cols(i):
            return slice(i * P, (i + 1) * P)

        def flip_w(b):
            w_words = w_rows[b][:].bitcast(F32).rearrange("o (t p u) -> o t u p", t=W_PART_ROWS, u=2)
            w_t = flip_banks.tile([P, W_PART_ROWS, 2, P], F32, tag="flip")
            for t in range(W_PART_ROWS):
                for u in range(2):
                    nc.tensor.transpose(w_t[:, t, u, :], w_words[:, t, u, :], identity[:])
            nc.scalar.copy(
                out=w_grouped_words[:, b * W_PART_ROWS : (b + 1) * W_PART_ROWS, :, :],
                in_=w_t[:].rearrange("p t u o -> p t o u"),
            )

        def quantise_w(b):
            words = slice(b * W_PART_ROWS * P, (b + 1) * W_PART_ROWS * P)
            values = slice(b * W_PART_ROWS * P * PACK, (b + 1) * W_PART_ROWS * P * PACK)
            nc.vector.quantize_mx(out=w_codes[:, words].bitcast(FP8X4), scales=w_scales[:, words], in_=w_grouped[:, values])

        def quantise(codes, scales, grouped, cols):
            nc.vector.quantize_mx(
                out=codes[:, cols].bitcast(FP8X4),
                scales=scales[:, cols],
                in_=grouped[:, cols, :].rearrange("p w j -> p (w j)"),
            )

        def quantise_seg(a, b):
            quantise(seg_codes, seg_scales, seg_grouped, slice(a, b))

        def quantise_q(h):
            quantise(q_codes, q_scales, q_grouped, half_cols[h])

        def regroup_seg(copy, k, a, b):
            first = SEG_PIECES[k][0]
            regroup(copy, seg_grouped[:, a:b, :], seg_rows[k][:, :, a - first : b - first])

        def regroup_q(copy, h, a, b):
            regroup(copy, q_grouped[:, h * BANK + a : h * BANK + b, :], q_rows[h][:, :, a:b])

        def project_keys(i):
            key_bank = key_banks.tile([P, PACK, P], F32, tag="key")
            for t in range(PACK):
                nc.tensor.matmul_mx(
                    out=key_bank[:, t, :],
                    lhsT=w_codes[:, t * P : (t + 1) * P].bitcast(FP8X4),
                    lhsT_scale=w_scales[:, t * P : (t + 1) * P],
                    rhs=seg_codes[:, m_cols(i)].bitcast(FP8X4),
                    rhs_scale=seg_scales[:, m_cols(i)],
                    start=True,
                    stop=True,
                )
            live["key_bank", i] = key_bank

        def add_bias(i):
            nc.vector.tensor_tensor(
                out=key_grouped[:, m_cols(i), :],
                in0=live["key_bank", i][:].rearrange("p t m -> p m t"),
                in1=bias[:].unsqueeze(1).to_broadcast([P, P, PACK]),
                op=ALU.add,
            )

        def quantise_key(i):
            quantise(key_codes, key_scales, key_grouped, m_cols(i))

        def score_half(i, h):
            score_bank = score_banks.tile([P, BANK], F32, tag="score")
            nc.tensor.matmul_mx(
                out=score_bank[:],
                lhsT=key_codes[:, m_cols(i)].bitcast(FP8X4),
                lhsT_scale=key_scales[:, m_cols(i)],
                rhs=q_codes[:, half_cols[h]].bitcast(FP8X4),
                rhs_scale=q_scales[:, half_cols[h]],
                start=True,
                stop=True,
            )
            live["score", i, h] = score_bank

        def score(i):
            for h in range(HALVES):
                score_half(i, h)

        def evacuate(i, h):
            if h == 0:
                row = rows_pool.tile([P, N], F32)
                mins = stats.tile([P, HALVES], F32)
                live["row", i] = row
                live["mins", i] = mins
            mins = live["mins", i]
            nc.vector.tensor_scalar(
                out=live["row", i][:, half_cols[h]],
                in0=live["score", i, h][:],
                scalar1=-1.0,
                scalar2=None if h == 0 else mins[:, h - 1 : h],
                op0=ALU.mult,
                op1=ALU.min,
                accum_out=mins[:, h : h + 1],
            )

        def exponentials(i):
            total = stats.tile([P, 1], F32)
            nc.scalar.activation(
                out=live["row", i][:],
                in_=live["row", i][:],
                func=ACT.Exp,
                bias=live["mins", i][:, HALVES - 1 : HALVES],
                scale=-1.0,
                accum_out=total[:],
            )
            live["total", i] = total

        def invert_sum(i):
            inverse = stats.tile([P, 1], F32)
            nc.vector.reciprocal(out=inverse[:], in_=live["total", i][:])
            live["inverse", i] = inverse

        def scale_on_gpsimd(i):
            row = live["row", i]
            for h in range(HALVES):
                nc.gpsimd.tensor_scalar(
                    out=row[:, half_cols[h]],
                    in0=row[:, half_cols[h]],
                    scalar1=live["inverse", i][:],
                    scalar2=0.0,
                    op0=ALU.mult,
                    op1=ALU.add,
                )

        def scale_on_vector(i):
            row = live["row", i]
            for h in range(HALVES):
                nc.vector.tensor_scalar(
                    out=row[:, half_cols[h]],
                    in0=row[:, half_cols[h]],
                    scalar1=live["inverse", i][:],
                    scalar2=None,
                    op0=ALU.mult,
                )

        def flip(i, banks, tag, halves=range(HALVES)):
            row = live["row", i]
            for h in halves:
                flipped = banks.tile([P, N_TILES_PER_BANK, P], F32, tag=tag)
                for j in range(N_TILES_PER_BANK):
                    n_tile = h * N_TILES_PER_BANK + j
                    nc.tensor.transpose(flipped[:, j, :], row[:, n_tile * P : (n_tile + 1) * P], identity[:])
                live["flipped", i, h] = flipped

        group_of = {}
        first = 0
        for size in STORE_GROUPS:
            for i in range(first, first + size):
                group_of[i] = (first, size)
            first += size

        def copy_out(copy, i, h, a=0, b=N_TILES_PER_BANK):
            first_tile, size = group_of[i]
            if ("staged", first_tile, h) not in live:
                staged = staging.tile([P, N_TILES_PER_BANK, size * P], F32, name="staged%d" % size)
                live["staged", first_tile, h] = staged
            staged = live["staged", first_tile, h]
            place = i - first_tile
            copy(out=staged[:, a:b, place * P : (place + 1) * P], in_=live["flipped", i, h][:, a:b, :])

        def store(i, h):
            first_tile, size = group_of[i]
            if i == first_tile + size - 1:
                n_tiles = slice(h * N_TILES_PER_BANK, (h + 1) * N_TILES_PER_BANK)
                nc.sync.dma_start(
                    out=out_dram[:, n_tiles, first_tile * P : (first_tile + size) * P],
                    in_=live["staged", first_tile, h][:],
                )

        on_vector = nc.vector.tensor_copy
        on_scalar = nc.scalar.copy

        keep_tensor_awake(3)
        for b in range(W_PARTS):
            flip_w(b)
        keep_tensor_awake(3)
        regroup_seg(on_vector, 0, 0, 256)
        quantise_w(0)
        quantise_seg(0, 256)
        regroup_q(on_scalar, 0, Q_VECTOR_COLS[0], BANK)
        regroup_q(on_vector, 0, 0, Q_VECTOR_COLS[0])
        quantise_w(1)
        project_keys(0)
        project_keys(1)
        keep_tensor_awake(4)
        regroup_q(on_scalar, 1, Q_VECTOR_COLS[1], BANK)
        quantise_q(0)
        regroup_q(on_vector, 1, 0, Q_VECTOR_COLS[1])
        add_bias(0)
        regroup_seg(on_scalar, 1, 256, 512)
        add_bias(1)
        quantise_key(0)
        score_half(0, 0)
        quantise_q(1)
        score_half(0, 1)
        quantise_seg(256, 512)
        regroup_seg(on_scalar, 2, 512, 768)

        def at(stage, i, *more):
            if 0 <= i < M_TILES:
                stage(i, *more)

        last = M_TILES - 1
        for s in range(-1, last):
            if s >= 2:
                flip(s - 2, flip_banks, "flip", (1,))
            if s >= 1:
                flip(s - 1, flip_banks, "flip", (0,))
            if s >= 0:
                at(add_bias, s + 2)
            at(evacuate, s + 1, 0)
            at(quantise_key, s + 2)
            if s == 1:
                quantise_seg(768, 1024)
            at(exponentials, s)
            if s == last - 1:
                copy_out(on_vector, s - 2, 1)
                store(s - 2, 1)
            if s <= LAST_GPSIMD_TILE:
                at(invert_sum, s)
                at(scale_on_gpsimd, s)
            at(evacuate, s + 1, 1)
            if s == -1:
                quantise_seg(512, 768)
            if s == 0:
                regroup_seg(on_scalar, 2, 768, 1024)
            at(project_keys, s + 3)
            at(score, s + 2)
            if 2 <= s < last - 1:
                copy_out(on_scalar, s - 2, 1)
                store(s - 2, 1)
            if 1 <= s < last:
                copy_out(on_scalar, s - 1, 0)
                store(s - 1, 0)

        exponentials(last)
        flip(last - 2, key_banks, "key", (1,))
        invert_sum(last - 1)
        scale_on_vector(last - 1)
        flip(last - 1, score_banks, "score")
        copy_out(on_vector, last - 2, 1)
        store(last - 2, 1)
        copy_out(on_scalar, last - 1, 0)
        store(last - 1, 0)
        invert_sum(last)
        scale_on_vector(last)
        flip(last, score_banks, "score")
        copy_out(on_scalar, last - 1, 1)
        store(last - 1, 1)
        copy_out(on_vector, last, 0)
        store(last, 0)
        copy_out(on_scalar, last, 1)
        store(last, 1)
